import numpy as np
import ml_dtypes


def mxq(x, axis, fmt="e4m3"):
    dtype, down = {"e4m3": (ml_dtypes.float8_e4m3fn, 7), "e5m2": (ml_dtypes.float8_e5m2, 14)}[fmt]
    v = np.moveaxis(np.asarray(x, np.float32).astype(ml_dtypes.bfloat16).astype(np.float64), axis, -1)
    blocks = v.reshape(v.shape[:-1] + (-1, 32))
    amax = np.abs(blocks).max(-1, keepdims=True)
    byte = np.maximum(np.where(amax > 0, np.frexp(amax)[1] - 1 + 127, 0) - down, 1)
    scale = np.exp2(byte - 127.0)
    codes = (blocks / scale).astype(np.float32).astype(dtype).astype(np.float64)
    return np.moveaxis((codes * scale).reshape(v.shape), -1, axis)


WIDE = False


def mx_kscale(k):
    if not WIDE:
        return np.ones(k)
    levels = np.array([10, -10, 5, -5, 0])
    a = np.random.permutation(np.resize(levels, k // 512 * 4)).reshape(k // 512, 4)
    idx = np.arange(k)
    return np.exp2(a[idx // 512, idx % 128 // 32])


BF16 = ml_dtypes.bfloat16


def bf(x):
    return np.asarray(x, np.float32).astype(BF16)


def f64(x):
    return np.asarray(x).astype(np.float64)


E2M1 = np.array([0.0, 0.5, 1.0, 1.5, 2.0, 3.0, 4.0, 6.0, -0.0, -0.5, -1.0, -1.5, -2.0, -3.0, -4.0, -6.0])


def pack_weight(w, fmt):
    k, n = w.shape
    w = f64(bf(w)).reshape(k // 32, 32, n)
    amax = np.abs(w).max(1)
    if fmt == "e4m3":
        byte = np.frexp(amax)[1] - 1 + 127 - 7
    else:
        mant, ex = np.frexp(amax / 6.0)
        byte = np.where(mant > 0.5, ex, ex - 1) + 127
    byte = np.clip(np.where(amax > 0, byte, 1), 1, 254)
    scaled = (w * np.exp2(127.0 - byte)[:, None, :]).reshape(k, n).astype(np.float32)
    by_word = np.ascontiguousarray(scaled.reshape(k // 512, 128, 4, n).transpose(0, 1, 3, 2))
    if fmt == "e4m3":
        words = by_word.astype(ml_dtypes.float8_e4m3fn).view(np.uint8)
    else:
        c = by_word.astype(ml_dtypes.float4_e2m1fn).view(np.uint8) & 0xF
        words = c[..., 0::2] | (c[..., 1::2] << 4)
    return np.ascontiguousarray(words), np.ascontiguousarray(byte.astype(np.uint8).reshape(k // 512, 16, n))


def unpack_weight(words, scales, fmt):
    g, p, n, _ = words.shape
    if fmt == "e4m3":
        vals = np.ascontiguousarray(words).view(ml_dtypes.float8_e4m3fn).astype(np.float64)
    else:
        nib = np.empty((g, p, n, 4), np.uint8)
        nib[..., 0::2] = words & 0xF
        nib[..., 1::2] = words >> 4
        vals = E2M1[nib]
    vals = vals * np.repeat(np.exp2(scales.astype(np.float64) - 127.0), 8, axis=1)[..., None]
    return vals.transpose(0, 1, 3, 2).reshape(g * 512, n)


B, S, HIDDEN, Q_LORA, NUM_HEADS, QK_NOPE, QK_ROPE, KV_LORA = 1, 128, 4096, 2048, 16, 128, 64, 1984
QK_HEAD = QK_NOPE + QK_ROPE


def rotate_half(t):
    d = t.shape[-1] // 2
    return np.concatenate([-t[..., d:], t[..., :d]], axis=-1)


def setup_inputs():
    s, t = mx_kscale(HIDDEN), mx_kscale(Q_LORA)
    x = bf(np.random.standard_normal((B, S, HIDDEN)) * s)
    cos = bf(np.random.uniform(size=(B, S, QK_ROPE)))
    sin = bf(np.random.uniform(size=(B, S, QK_ROPE)))
    Wqa = np.random.standard_normal((Q_LORA, HIDDEN)) / np.sqrt(HIDDEN) * t[:, None] / s
    Wqb = np.random.standard_normal((NUM_HEADS * QK_HEAD, Q_LORA)) / np.sqrt(Q_LORA) / t
    Wkva = np.random.standard_normal((KV_LORA + QK_ROPE, HIDDEN)) / np.sqrt(HIDDEN) / s
    Wqa_words, Wqa_scales = pack_weight(np.ascontiguousarray(Wqa.T), "e4m3")
    Wqb_words, Wqb_scales = pack_weight(np.ascontiguousarray(Wqb.T), "e4m3")
    Wkva_words, Wkva_scales = pack_weight(np.ascontiguousarray(Wkva.T), "e4m3")
    return {"x": x, "cos": cos, "sin": sin, "Wqa_words": Wqa_words, "Wqa_scales": Wqa_scales, "Wqb_words": Wqb_words, "Wqb_scales": Wqb_scales, "Wkva_words": Wkva_words, "Wkva_scales": Wkva_scales}


def reference(x, cos, sin, Wqa_words, Wqa_scales, Wqb_words, Wqb_scales, Wkva_words, Wkva_scales):
    b, s, _ = x.shape
    xq = mxq(f64(x), 2, "e4m3")
    qa = xq @ unpack_weight(Wqa_words, Wqa_scales, "e4m3")
    q = (mxq(qa, 2, "e4m3") @ unpack_weight(Wqb_words, Wqb_scales, "e4m3")).reshape(b, s, NUM_HEADS, QK_HEAD)
    q_nope = q[..., :QK_NOPE]
    q_pe = q[..., QK_NOPE:]
    kv = xq @ unpack_weight(Wkva_words, Wkva_scales, "e4m3")
    compressed_kv = kv[..., :KV_LORA]
    k_pe = kv[..., KV_LORA:].reshape(b, s, 1, QK_ROPE)
    c = f64(cos)[:, :, None, :]
    sn = f64(sin)[:, :, None, :]
    q_pe_rot = q_pe * c + rotate_half(q_pe) * sn
    k_pe_rot = k_pe * c + rotate_half(k_pe) * sn
    q_out = np.concatenate([q_nope, q_pe_rot], axis=-1).reshape(b, s, -1)
    k_out = k_pe_rot.reshape(b, s, QK_ROPE)
    return np.concatenate([q_out, k_out, compressed_kv], axis=-1)

@@ -1,0 +1,238 @@
+from contextlib import ExitStack
+
+import concourse.mybir as mybir
+from concourse.masks import make_identity
+
+F32 = mybir.dt.float32
+BF16 = mybir.dt.bfloat16
+I32 = mybir.dt.int32
+U32 = mybir.dt.uint32
+U8 = mybir.dt.uint8
+FP8X4 = mybir.dt.float8_e4m3fn_x4
+
+P = 128
+FLOPS = 2 * 128 * (4096 * 2048 * 2 + 2048 * 3072)
+
+SCALE_QUEUE_A = "sync"
+SCALE_QUEUE_B = "sync"
+SCALE_QUEUE_K = "sync"
+W8_BUFS = 10
+KV_AHEAD = 2
+
+
+def tile_mlaselfattn_w_kernel(
+    tc, x, cos, sin, Wqa_words, Wqa_scales, Wqb_words, Wqb_scales, Wkva_words, Wkva_scales, out
+):
+    nc = tc.nc
+    x2 = x.rearrange("b s h -> (b s) h")
+    cos2 = cos.rearrange("b s d -> (b s) d")
+    sin2 = sin.rearrange("b s d -> (b s) d")
+    out2 = out.rearrange("b s n -> (b s) n")
+    wqa_v = Wqa_words.rearrange("g p n t -> g p (n t)").bitcast(I32)
+    wqb_v = Wqb_words.rearrange("g p n t -> g p (n t)").bitcast(I32)
+    wkv_v = Wkva_words.rearrange("g p n t -> g p (n t)").bitcast(I32)
+
+    with ExitStack() as ctx:
+        keep = ctx.enter_context(tc.tile_pool(name="keep", bufs=1))
+        w8 = ctx.enter_context(tc.tile_pool(name="w8", bufs=W8_BUFS))
+        w12 = ctx.enter_context(tc.tile_pool(name="w12", bufs=4))
+        wh = ctx.enter_context(tc.tile_pool(name="wh", bufs=2))
+        tmpp = ctx.enter_context(tc.tile_pool(name="tmpp", bufs=2))
+        ps = ctx.enter_context(tc.psum_pool(name="ps", bufs=1))
+        ctx.enter_context(tc.manual_schedule())
+
+        def bank(i, shape, dtype, name):
+            return ps.tile(shape, dtype, tag="b%d" % i, name=name)
+
+        ident_f = keep.tile([P, P], F32, name="ident_f")
+        ident_b = keep.tile([P, P], BF16, name="ident_b")
+        pl_a = keep.tile([P, 4096], U8, name="pl_a", align_bytes=64)
+        pl_b = keep.tile([P, 3072], U8, name="pl_b", align_bytes=64)
+        pl_k = keep.tile([P, 4096], U8, name="pl_k", align_bytes=64)
+        x_sb = keep.tile([P, 4096], BF16, name="x_sb", align_bytes=64)
+        cos_b = keep.tile([P, 64], BF16, name="cos_b")
+        sin_b = keep.tile([P, 64], BF16, name="sin_b")
+        cos_f = keep.tile([P, 64], F32, name="cos_f")
+        sin_s = keep.tile([P, 64], F32, name="sin_s")
+        xg = keep.tile([P, 4096], BF16, name="xg", align_bytes=64)
+        xw = keep.tile([P, 1024], U32, name="xw", align_bytes=64)
+        xs = keep.tile([P, 1024], U8, name="xs", align_bytes=64)
+        qs = keep.tile([P, 4, 4, P], BF16, name="qs", align_bytes=64)
+        qg = keep.tile([P, 2048], BF16, name="qg", align_bytes=64)
+        qw = keep.tile([P, 512], U32, name="qw", align_bytes=64)
+        qsc = keep.tile([P, 512], U8, name="qsc", align_bytes=64)
+        o_q = keep.tile([P, 3072], F32, name="o_q")
+        o_kv = keep.tile([P, 2048], F32, name="o_kv")
+        tmp_k = keep.tile([P, 64], F32, name="tmp_k")
+
+        make_identity(nc, ident_f[:])
+        nc.vector.memset(pl_a[:].bitcast(I32), 0)
+        nc.vector.memset(pl_b[:].bitcast(I32), 0)
+        nc.vector.memset(pl_k[:].bitcast(I32), 0)
+
+        nc.sync.dma_start(out=x_sb[:], in_=x2)
+        nc.sync.dma_start(out=cos_b[:], in_=cos2)
+        nc.sync.dma_start(out=sin_b[:], in_=sin2)
+
+        def load_planes(which, planes, scales, groups, width):
+            if which == "sync":
+                queue, view = nc.sync, I32
+            else:
+                queue, view = nc.gpsimd, F32
+            sv = scales.bitcast(view)
+            for a in range(groups // 4):
+                for quad in (0, 2, 1, 3):
+                    queue.dma_start(
+                        out=planes[32 * quad : 32 * quad + 16, a * width : (a + 1) * width].bitcast(view),
+                        in_=sv[4 * a : 4 * a + 4, 4 * quad : 4 * quad + 4, :],
+                    )
+
+        load_planes(SCALE_QUEUE_A, pl_a, Wqa_scales, 8, 2048)
+        load_planes(SCALE_QUEUE_B, pl_b, Wqb_scales, 4, 3072)
+        load_planes(SCALE_QUEUE_K, pl_k, Wkva_scales, 8, 2048)
+        make_identity(nc, ident_b[:])
+
+        wqa_t = {}
+        wqb_t = {}
+        wkv_t = {}
+
+        def load_qa(g):
+            t = w8.tile([P, 2048], U32, tag="w8", name="wqa%d" % g, align_bytes=64)
+            nc.sync.dma_start(out=t[:].bitcast(I32), in_=wqa_v[g])
+            wqa_t[g] = t
+
+        def load_qb(g):
+            t = w12.tile([P, 3072], U32, tag="w12", name="wqb%d" % g, align_bytes=64)
+            nc.sync.dma_start(out=t[:].bitcast(I32), in_=wqb_v[g])
+            wqb_t[g] = t
+
+        def load_kv(g):
+            t = w8.tile([P, 2048], U32, tag="w8", name="wkv%d" % g, align_bytes=64)
+            nc.sync.dma_start(out=t[:].bitcast(I32), in_=wkv_v[g])
+            wkv_t[g] = t
+
+        def load_kv_halves():
+            for h in (1, 0):
+                t = wh.tile([P, 1024], U32, tag="wh", name="wkv7h%d" % h, align_bytes=64)
+                nc.sync.dma_start(out=t[:].bitcast(I32), in_=wkv_v[7][:, 1024 * h : 1024 * (h + 1)])
+                wkv_t[(7, h)] = t
+
+        for g in range(8):
+            load_qa(g)
+        for g in range(4):
+            load_qb(g)
+        for g in range(KV_AHEAD):
+            load_kv(g)
+
+        x_f = x_sb[:].bitcast(F32)
+        xg_f = xg[:].bitcast(F32)
+        for i in range(4):
+            xt = bank(4 + i, [P, 2, 2, P], F32, "xt%d" % i)
+            for gg in range(2):
+                g = 2 * i + gg
+                for u in range(2):
+                    nc.tensor.transpose(xt[:, gg, u, :], x_f[:, 256 * g + u : 256 * (g + 1) : 2], ident_f[:])
+            dst = xg_f[:, 512 * i : 512 * (i + 1)].rearrange("p (g r u) -> p g r u", g=2, u=2)
+            src = xt[:].rearrange("p g u r -> p g r u")
+            if i % 2 == 0:
+                nc.vector.tensor_copy(out=dst, in_=src)
+            else:
+                nc.scalar.copy(out=dst, in_=src)
+        for h in range(2):
+            nc.vector.quantize_mx(
+                out=xw[:, 512 * h : 512 * (h + 1)].bitcast(FP8X4),
+                scales=xs[:, 512 * h : 512 * (h + 1)],
+                in_=xg[:, 2048 * h : 2048 * (h + 1)],
+            )
+        nc.vector.tensor_copy(out=cos_f[:], in_=cos_b[:])
+        nc.vector.tensor_scalar_mul(out=sin_s[:, 0:32], in0=sin_b[:, 0:32], scalar1=-1.0)
+        nc.vector.tensor_copy(out=sin_s[:, 32:64], in_=sin_b[:, 32:64])
+
+        def mx(acc, lw, ls, g, wt, wcols, planes, off, pcols, start, stop):
+            nc.tensor.matmul_mx(
+                out=acc,
+                lhsT=lw[:, P * g : P * (g + 1)].bitcast(FP8X4),
+                lhsT_scale=ls[:, P * g : P * (g + 1)],
+                rhs=wt[:, wcols].bitcast(FP8X4),
+                rhs_scale=planes[off:P, pcols],
+                start=start,
+                stop=stop,
+            )
+
+        qa_ps = [bank(j, [P, 512], F32, "qa_ps%d" % j) for j in range(4)]
+        for g in range(8):
+            base = 2048 * (g // 4)
+            for j in range(4):
+                mx(qa_ps[j][:], xw, xs, g, wqa_t[g], slice(512 * j, 512 * (j + 1)), pl_a, 4 * (g % 4),
+                   slice(base + 512 * j, base + 512 * (j + 1)), g == 0, g == 7)
+            nxt = g + KV_AHEAD
+            if nxt < 7:
+                load_kv(nxt)
+            elif nxt == 7:
+                load_kv_halves()
+
+        for g in range(4):
+            src = qa_ps[g][:].rearrange("r (p t) -> r t p", t=4)
+            if g % 2 == 0:
+                nc.vector.tensor_copy(out=qs[:, g], in_=src)
+            else:
+                nc.scalar.copy(out=qs[:, g], in_=src)
+        qg4 = qg[:].rearrange("p (g r t) -> p g r t", g=4, t=4)
+        for g in range(4):
+            qt = bank(4 + g, [P, 4, P], BF16, "qt%d" % g)
+            for t in range(4):
+                nc.tensor.transpose(qt[:, t, :], qs[:, g, t, :], ident_b[:])
+            src = qt[:].rearrange("p t r -> p r t")
+            if g % 2 == 0:
+                nc.vector.tensor_copy(out=qg4[:, g], in_=src)
+            else:
+                nc.scalar.copy(out=qg4[:, g], in_=src)
+        nc.vector.quantize_mx(out=qw[:].bitcast(FP8X4), scales=qsc[:], in_=qg[:])
+
+        q_ps = [bank(b, [P, 512], F32, "q_ps%d" % b) for b in range(6)]
+        for g in range(4):
+            for b in range(6):
+                cols = slice(512 * b, 512 * (b + 1))
+                mx(q_ps[b][:], qw, qsc, g, wqb_t[g], cols, pl_b, 4 * g, cols, g == 0, g == 3)
+        for b in range(6):
+            if b % 2 == 0:
+                nc.scalar.copy(out=o_q[:, 512 * b : 512 * (b + 1)], in_=q_ps[b][:])
+            else:
+                nc.vector.tensor_copy(out=o_q[:, 512 * b : 512 * (b + 1)], in_=q_ps[b][:])
+        oq3 = o_q[:].rearrange("p (h d) -> p h d", d=192)
+        for half in range(2):
+            hs = slice(8 * half, 8 * (half + 1))
+            tmp = tmpp.tile([P, 8, 64], F32, tag="tmp", name="tmp%d" % half)
+            nc.vector.tensor_mul(out=tmp[:, :, 0:32], in0=oq3[:, hs, 160:192],
+                                 in1=sin_s[:, 0:32].unsqueeze(1).to_broadcast([P, 8, 32]))
+            nc.vector.tensor_mul(out=tmp[:, :, 32:64], in0=oq3[:, hs, 128:160],
+                                 in1=sin_s[:, 32:64].unsqueeze(1).to_broadcast([P, 8, 32]))
+            nc.vector.tensor_mul(out=oq3[:, hs, 128:192], in0=oq3[:, hs, 128:192],
+                                 in1=cos_f[:].unsqueeze(1).to_broadcast([P, 8, 64]))
+            nc.vector.tensor_add(out=oq3[:, hs, 128:192], in0=oq3[:, hs, 128:192], in1=tmp[:])
+        nc.sync.dma_start(out=out2[:, 0:3072], in_=o_q[:])
+
+        kv_bank = (6, 7, 0, 1)
+        kv_ps = [bank(kv_bank[j], [P, 512], F32, "kv_ps%d" % j) for j in range(4)]
+        for g in range(7):
+            base = 2048 * (g // 4)
+            for j in range(4):
+                mx(kv_ps[j][:], xw, xs, g, wkv_t[g], slice(512 * j, 512 * (j + 1)), pl_k, 4 * (g % 4),
+                   slice(base + 512 * j, base + 512 * (j + 1)), g == 0, False)
+        for h in (1, 0):
+            for jj in range(2):
+                j = 2 * h + jj
+                mx(kv_ps[j][:], xw, xs, 7, wkv_t[(7, h)], slice(512 * jj, 512 * (jj + 1)), pl_k, 12,
+                   slice(2048 + 512 * j, 2048 + 512 * (j + 1)), False, True)
+            if h == 1:
+                nc.scalar.copy(out=o_kv[:, 1088:1600], in_=kv_ps[2][:])
+                nc.vector.tensor_copy(out=o_kv[:, 1600:2048], in_=kv_ps[3][:, 0:448])
+                nc.vector.tensor_mul(out=tmp_k[:, 0:32], in0=kv_ps[3][:, 480:512], in1=sin_s[:, 0:32])
+                nc.vector.tensor_mul(out=tmp_k[:, 32:64], in0=kv_ps[3][:, 448:480], in1=sin_s[:, 32:64])
+                nc.vector.tensor_mul(out=o_kv[:, 0:64], in0=kv_ps[3][:, 448:512], in1=cos_f[:])
+                nc.vector.tensor_add(out=o_kv[:, 0:64], in0=o_kv[:, 0:64], in1=tmp_k[:])
+                nc.sync.dma_start(out=out2[:, 3072 + 1088 : 5120], in_=o_kv[:, 1088:2048])
+            else:
+                nc.scalar.copy(out=o_kv[:, 64:576], in_=kv_ps[0][:])
+                nc.vector.tensor_copy(out=o_kv[:, 576:1088], in_=kv_ps[1][:])
+                nc.sync.dma_start(out=out2[:, 3072 : 3072 + 1088], in_=o_kv[:, 0:1088])

@@ -13,9 +13,9 @@ FP8X4 = mybir.dt.float8_e4m3fn_x4
 P = 128
 FLOPS = 2 * 128 * (4096 * 2048 * 2 + 2048 * 3072)
 
-SCALE_QUEUE_A = "sync"
-SCALE_QUEUE_B = "sync"
-SCALE_QUEUE_K = "sync"
+SCALE_QUEUE_A = "gpsimd"
+SCALE_QUEUE_B = "gpsimd"
+SCALE_QUEUE_K = "gpsimd"
 W8_BUFS = 10
 KV_AHEAD = 2
 
@@ -88,9 +88,9 @@ def tile_mlaselfattn_w_kernel(
                     )
 
         load_planes(SCALE_QUEUE_A, pl_a, Wqa_scales, 8, 2048)
+        make_identity(nc, ident_b[:])
         load_planes(SCALE_QUEUE_B, pl_b, Wqb_scales, 4, 3072)
         load_planes(SCALE_QUEUE_K, pl_k, Wkva_scales, 8, 2048)
-        make_identity(nc, ident_b[:])
 
         wqa_t = {}
         wqb_t = {}

@@ -13,9 +13,6 @@ FP8X4 = mybir.dt.float8_e4m3fn_x4
 P = 128
 FLOPS = 2 * 128 * (4096 * 2048 * 2 + 2048 * 3072)
 
-SCALE_QUEUE_A = "gpsimd"
-SCALE_QUEUE_B = "gpsimd"
-SCALE_QUEUE_K = "gpsimd"
 W8_BUFS = 10
 KV_AHEAD = 2
 
@@ -71,26 +68,16 @@ def tile_mlaselfattn_w_kernel(
         nc.vector.memset(pl_k[:].bitcast(I32), 0)
 
         nc.sync.dma_start(out=x_sb[:], in_=x2)
-        nc.sync.dma_start(out=cos_b[:], in_=cos2)
-        nc.sync.dma_start(out=sin_b[:], in_=sin2)
 
-        def load_planes(which, planes, scales, groups, width):
-            if which == "sync":
-                queue, view = nc.sync, I32
-            else:
-                queue, view = nc.gpsimd, F32
-            sv = scales.bitcast(view)
-            for a in range(groups // 4):
-                for quad in (0, 2, 1, 3):
-                    queue.dma_start(
-                        out=planes[32 * quad : 32 * quad + 16, a * width : (a + 1) * width].bitcast(view),
-                        in_=sv[4 * a : 4 * a + 4, 4 * quad : 4 * quad + 4, :],
-                    )
+        def load_planes(planes, scales, a, width, quads):
+            sv = scales.bitcast(I32)
+            for quad in quads:
+                nc.sync.dma_start(
+                    out=planes[32 * quad : 32 * quad + 16, a * width : (a + 1) * width].bitcast(I32),
+                    in_=sv[4 * a : 4 * a + 4, 4 * quad : 4 * quad + 4, :],
+                )
 
-        load_planes(SCALE_QUEUE_A, pl_a, Wqa_scales, 8, 2048)
         make_identity(nc, ident_b[:])
-        load_planes(SCALE_QUEUE_B, pl_b, Wqb_scales, 4, 3072)
-        load_planes(SCALE_QUEUE_K, pl_k, Wkva_scales, 8, 2048)
 
         wqa_t = {}
         wqb_t = {}
@@ -117,7 +104,25 @@ def tile_mlaselfattn_w_kernel(
                 nc.sync.dma_start(out=t[:].bitcast(I32), in_=wkv_v[7][:, 1024 * h : 1024 * (h + 1)])
                 wkv_t[(7, h)] = t
 
-        for g in range(8):
+        upper = (2, 3)
+        lower = (0, 1)
+        load_planes(pl_a, Wqa_scales, 0, 2048, upper)
+        load_planes(pl_a, Wqa_scales, 1, 2048, upper)
+        load_planes(pl_b, Wqb_scales, 0, 3072, upper)
+        load_planes(pl_k, Wkva_scales, 0, 2048, upper)
+        load_planes(pl_k, Wkva_scales, 1, 2048, upper)
+        load_planes(pl_a, Wqa_scales, 0, 2048, lower)
+        load_planes(pl_a, Wqa_scales, 1, 2048, lower)
+        load_qa(0)
+        load_planes(pl_b, Wqb_scales, 0, 3072, lower)
+        load_qa(1)
+        load_planes(pl_k, Wkva_scales, 0, 2048, lower)
+        load_qa(2)
+        load_planes(pl_k, Wkva_scales, 1, 2048, lower)
+        load_qa(3)
+        nc.sync.dma_start(out=cos_b[:], in_=cos2)
+        nc.sync.dma_start(out=sin_b[:], in_=sin2)
+        for g in range(4, 8):
             load_qa(g)
         for g in range(4):
             load_qb(g)

from contextlib import ExitStack

import concourse.mybir as mybir
from concourse.masks import make_identity

F32 = mybir.dt.float32
BF16 = mybir.dt.bfloat16
I32 = mybir.dt.int32
U32 = mybir.dt.uint32
U8 = mybir.dt.uint8
FP8X4 = mybir.dt.float8_e4m3fn_x4

P = 128
FLOPS = 2 * 128 * (4096 * 2048 * 2 + 2048 * 3072)

W8_BUFS = 10
KV_AHEAD = 2


def tile_mlaselfattn_w_kernel(
    tc, x, cos, sin, Wqa_words, Wqa_scales, Wqb_words, Wqb_scales, Wkva_words, Wkva_scales, out
):
    nc = tc.nc
    x2 = x.rearrange("b s h -> (b s) h")
    cos2 = cos.rearrange("b s d -> (b s) d")
    sin2 = sin.rearrange("b s d -> (b s) d")
    out2 = out.rearrange("b s n -> (b s) n")
    wqa_v = Wqa_words.rearrange("g p n t -> g p (n t)").bitcast(I32)
    wqb_v = Wqb_words.rearrange("g p n t -> g p (n t)").bitcast(I32)
    wkv_v = Wkva_words.rearrange("g p n t -> g p (n t)").bitcast(I32)

    with ExitStack() as ctx:
        keep = ctx.enter_context(tc.tile_pool(name="keep", bufs=1))
        w8 = ctx.enter_context(tc.tile_pool(name="w8", bufs=W8_BUFS))
        w12 = ctx.enter_context(tc.tile_pool(name="w12", bufs=4))
        wh = ctx.enter_context(tc.tile_pool(name="wh", bufs=2))
        tmpp = ctx.enter_context(tc.tile_pool(name="tmpp", bufs=2))
        ps = ctx.enter_context(tc.psum_pool(name="ps", bufs=1))
        ctx.enter_context(tc.manual_schedule())

        def bank(i, shape, dtype, name):
            return ps.tile(shape, dtype, tag="b%d" % i, name=name)

        ident_f = keep.tile([P, P], F32, name="ident_f")
        ident_b = keep.tile([P, P], BF16, name="ident_b")
        pl_a = keep.tile([P, 4096], U8, name="pl_a", align_bytes=64)
        pl_b = keep.tile([P, 3072], U8, name="pl_b", align_bytes=64)
        pl_k = keep.tile([P, 4096], U8, name="pl_k", align_bytes=64)
        x_sb = keep.tile([P, 4096], BF16, name="x_sb", align_bytes=64)
        cos_b = keep.tile([P, 64], BF16, name="cos_b")
        sin_b = keep.tile([P, 64], BF16, name="sin_b")
        cos_f = keep.tile([P, 64], F32, name="cos_f")
        sin_s = keep.tile([P, 64], F32, name="sin_s")
        xg = keep.tile([P, 4096], BF16, name="xg", align_bytes=64)
        xw = keep.tile([P, 1024], U32, name="xw", align_bytes=64)
        xs = keep.tile([P, 1024], U8, name="xs", align_bytes=64)
        qs = keep.tile([P, 4, 4, P], BF16, name="qs", align_bytes=64)
        qg = keep.tile([P, 2048], BF16, name="qg", align_bytes=64)
        qw = keep.tile([P, 512], U32, name="qw", align_bytes=64)
        qsc = keep.tile([P, 512], U8, name="qsc", align_bytes=64)
        o_q = keep.tile([P, 3072], F32, name="o_q")
        o_kv = keep.tile([P, 2048], F32, name="o_kv")
        tmp_k = keep.tile([P, 64], F32, name="tmp_k")

        make_identity(nc, ident_f[:])
        nc.vector.memset(pl_a[:].bitcast(I32), 0)
        nc.vector.memset(pl_b[:].bitcast(I32), 0)
        nc.vector.memset(pl_k[:].bitcast(I32), 0)

        nc.sync.dma_start(out=x_sb[:], in_=x2)

        def load_planes(planes, scales, a, width, quads):
            sv = scales.bitcast(I32)
            for quad in quads:
                nc.sync.dma_start(
                    out=planes[32 * quad : 32 * quad + 16, a * width : (a + 1) * width].bitcast(I32),
                    in_=sv[4 * a : 4 * a + 4, 4 * quad : 4 * quad + 4, :],
                )

        make_identity(nc, ident_b[:])

        wqa_t = {}
        wqb_t = {}
        wkv_t = {}

        def load_qa(g):
            t = w8.tile([P, 2048], U32, tag="w8", name="wqa%d" % g, align_bytes=64)
            nc.sync.dma_start(out=t[:].bitcast(I32), in_=wqa_v[g])
            wqa_t[g] = t

        def load_qb(g):
            t = w12.tile([P, 3072], U32, tag="w12", name="wqb%d" % g, align_bytes=64)
            nc.sync.dma_start(out=t[:].bitcast(I32), in_=wqb_v[g])
            wqb_t[g] = t

        def load_kv(g):
            t = w8.tile([P, 2048], U32, tag="w8", name="wkv%d" % g, align_bytes=64)
            nc.sync.dma_start(out=t[:].bitcast(I32), in_=wkv_v[g])
            wkv_t[g] = t

        def load_kv_halves():
            for h in (1, 0):
                t = wh.tile([P, 1024], U32, tag="wh", name="wkv7h%d" % h, align_bytes=64)
                nc.sync.dma_start(out=t[:].bitcast(I32), in_=wkv_v[7][:, 1024 * h : 1024 * (h + 1)])
                wkv_t[(7, h)] = t

        upper = (2, 3)
        lower = (0, 1)
        load_planes(pl_a, Wqa_scales, 0, 2048, upper)
        load_planes(pl_a, Wqa_scales, 1, 2048, upper)
        load_planes(pl_b, Wqb_scales, 0, 3072, upper)
        load_planes(pl_k, Wkva_scales, 0, 2048, upper)
        load_planes(pl_k, Wkva_scales, 1, 2048, upper)
        load_planes(pl_a, Wqa_scales, 0, 2048, lower)
        load_planes(pl_a, Wqa_scales, 1, 2048, lower)
        load_qa(0)
        load_planes(pl_b, Wqb_scales, 0, 3072, lower)
        load_qa(1)
        load_planes(pl_k, Wkva_scales, 0, 2048, lower)
        load_qa(2)
        load_planes(pl_k, Wkva_scales, 1, 2048, lower)
        load_qa(3)
        nc.sync.dma_start(out=cos_b[:], in_=cos2)
        nc.sync.dma_start(out=sin_b[:], in_=sin2)
        for g in range(4, 8):
            load_qa(g)
        for g in range(4):
            load_qb(g)
        for g in range(KV_AHEAD):
            load_kv(g)

        x_f = x_sb[:].bitcast(F32)
        xg_f = xg[:].bitcast(F32)
        for i in range(4):
            xt = bank(4 + i, [P, 2, 2, P], F32, "xt%d" % i)
            for gg in range(2):
                g = 2 * i + gg
                for u in range(2):
                    nc.tensor.transpose(xt[:, gg, u, :], x_f[:, 256 * g + u : 256 * (g + 1) : 2], ident_f[:])
            dst = xg_f[:, 512 * i : 512 * (i + 1)].rearrange("p (g r u) -> p g r u", g=2, u=2)
            src = xt[:].rearrange("p g u r -> p g r u")
            if i % 2 == 0:
                nc.vector.tensor_copy(out=dst, in_=src)
            else:
                nc.scalar.copy(out=dst, in_=src)
        for h in range(2):
            nc.vector.quantize_mx(
                out=xw[:, 512 * h : 512 * (h + 1)].bitcast(FP8X4),
                scales=xs[:, 512 * h : 512 * (h + 1)],
                in_=xg[:, 2048 * h : 2048 * (h + 1)],
            )
        nc.vector.tensor_copy(out=cos_f[:], in_=cos_b[:])
        nc.vector.tensor_scalar_mul(out=sin_s[:, 0:32], in0=sin_b[:, 0:32], scalar1=-1.0)
        nc.vector.tensor_copy(out=sin_s[:, 32:64], in_=sin_b[:, 32:64])

        def mx(acc, lw, ls, g, wt, wcols, planes, off, pcols, start, stop):
            nc.tensor.matmul_mx(
                out=acc,
                lhsT=lw[:, P * g : P * (g + 1)].bitcast(FP8X4),
                lhsT_scale=ls[:, P * g : P * (g + 1)],
                rhs=wt[:, wcols].bitcast(FP8X4),
                rhs_scale=planes[off:P, pcols],
                start=start,
                stop=stop,
            )

        qa_ps = [bank(j, [P, 512], F32, "qa_ps%d" % j) for j in range(4)]
        for g in range(8):
            base = 2048 * (g // 4)
            for j in range(4):
                mx(qa_ps[j][:], xw, xs, g, wqa_t[g], slice(512 * j, 512 * (j + 1)), pl_a, 4 * (g % 4),
                   slice(base + 512 * j, base + 512 * (j + 1)), g == 0, g == 7)
            nxt = g + KV_AHEAD
            if nxt < 7:
                load_kv(nxt)
            elif nxt == 7:
                load_kv_halves()

        for g in range(4):
            src = qa_ps[g][:].rearrange("r (p t) -> r t p", t=4)
            if g % 2 == 0:
                nc.vector.tensor_copy(out=qs[:, g], in_=src)
            else:
                nc.scalar.copy(out=qs[:, g], in_=src)
        qg4 = qg[:].rearrange("p (g r t) -> p g r t", g=4, t=4)
        for g in range(4):
            qt = bank(4 + g, [P, 4, P], BF16, "qt%d" % g)
            for t in range(4):
                nc.tensor.transpose(qt[:, t, :], qs[:, g, t, :], ident_b[:])
            src = qt[:].rearrange("p t r -> p r t")
            if g % 2 == 0:
                nc.vector.tensor_copy(out=qg4[:, g], in_=src)
            else:
                nc.scalar.copy(out=qg4[:, g], in_=src)
        nc.vector.quantize_mx(out=qw[:].bitcast(FP8X4), scales=qsc[:], in_=qg[:])

        q_ps = [bank(b, [P, 512], F32, "q_ps%d" % b) for b in range(6)]
        for g in range(4):
            for b in range(6):
                cols = slice(512 * b, 512 * (b + 1))
                mx(q_ps[b][:], qw, qsc, g, wqb_t[g], cols, pl_b, 4 * g, cols, g == 0, g == 3)
        for b in range(6):
            if b % 2 == 0:
                nc.scalar.copy(out=o_q[:, 512 * b : 512 * (b + 1)], in_=q_ps[b][:])
            else:
                nc.vector.tensor_copy(out=o_q[:, 512 * b : 512 * (b + 1)], in_=q_ps[b][:])
        oq3 = o_q[:].rearrange("p (h d) -> p h d", d=192)
        for half in range(2):
            hs = slice(8 * half, 8 * (half + 1))
            tmp = tmpp.tile([P, 8, 64], F32, tag="tmp", name="tmp%d" % half)
            nc.vector.tensor_mul(out=tmp[:, :, 0:32], in0=oq3[:, hs, 160:192],
                                 in1=sin_s[:, 0:32].unsqueeze(1).to_broadcast([P, 8, 32]))
            nc.vector.tensor_mul(out=tmp[:, :, 32:64], in0=oq3[:, hs, 128:160],
                                 in1=sin_s[:, 32:64].unsqueeze(1).to_broadcast([P, 8, 32]))
            nc.vector.tensor_mul(out=oq3[:, hs, 128:192], in0=oq3[:, hs, 128:192],
                                 in1=cos_f[:].unsqueeze(1).to_broadcast([P, 8, 64]))
            nc.vector.tensor_add(out=oq3[:, hs, 128:192], in0=oq3[:, hs, 128:192], in1=tmp[:])
        nc.sync.dma_start(out=out2[:, 0:3072], in_=o_q[:])

        kv_bank = (6, 7, 0, 1)
        kv_ps = [bank(kv_bank[j], [P, 512], F32, "kv_ps%d" % j) for j in range(4)]
        for g in range(7):
            base = 2048 * (g // 4)
            for j in range(4):
                mx(kv_ps[j][:], xw, xs, g, wkv_t[g], slice(512 * j, 512 * (j + 1)), pl_k, 4 * (g % 4),
                   slice(base + 512 * j, base + 512 * (j + 1)), g == 0, False)
        for h in (1, 0):
            for jj in range(2):
                j = 2 * h + jj
                mx(kv_ps[j][:], xw, xs, 7, wkv_t[(7, h)], slice(512 * jj, 512 * (jj + 1)), pl_k, 12,
                   slice(2048 + 512 * j, 2048 + 512 * (j + 1)), False, True)
            if h == 1:
                nc.scalar.copy(out=o_kv[:, 1088:1600], in_=kv_ps[2][:])
                nc.vector.tensor_copy(out=o_kv[:, 1600:2048], in_=kv_ps[3][:, 0:448])
                nc.vector.tensor_mul(out=tmp_k[:, 0:32], in0=kv_ps[3][:, 480:512], in1=sin_s[:, 0:32])
                nc.vector.tensor_mul(out=tmp_k[:, 32:64], in0=kv_ps[3][:, 448:480], in1=sin_s[:, 32:64])
                nc.vector.tensor_mul(out=o_kv[:, 0:64], in0=kv_ps[3][:, 448:512], in1=cos_f[:])
                nc.vector.tensor_add(out=o_kv[:, 0:64], in0=o_kv[:, 0:64], in1=tmp_k[:])
                nc.sync.dma_start(out=out2[:, 3072 + 1088 : 5120], in_=o_kv[:, 1088:2048])
            else:
                nc.scalar.copy(out=o_kv[:, 64:576], in_=kv_ps[0][:])
                nc.vector.tensor_copy(out=o_kv[:, 576:1088], in_=kv_ps[1][:])
                nc.sync.dma_start(out=out2[:, 3072 : 3072 + 1088], in_=o_kv[:, 0:1088])
